import numpy as np
import ml_dtypes


def mxq(x, axis, fmt="e4m3"):
    dtype, down = {"e4m3": (ml_dtypes.float8_e4m3fn, 7), "e5m2": (ml_dtypes.float8_e5m2, 14)}[fmt]
    v = np.moveaxis(np.asarray(x, np.float32).astype(ml_dtypes.bfloat16).astype(np.float64), axis, -1)
    blocks = v.reshape(v.shape[:-1] + (-1, 32))
    amax = np.abs(blocks).max(-1, keepdims=True)
    byte = np.maximum(np.where(amax > 0, np.frexp(amax)[1] - 1 + 127, 0) - down, 1)
    scale = np.exp2(byte - 127.0)
    codes = (blocks / scale).astype(np.float32).astype(dtype).astype(np.float64)
    return np.moveaxis((codes * scale).reshape(v.shape), -1, axis)


WIDE = False


def mx_kscale(k):
    if not WIDE:
        return np.ones(k)
    levels = np.array([20, -20, 10, -10, 0])
    a = np.random.permutation(np.resize(levels, k // 512 * 4)).reshape(k // 512, 4)
    idx = np.arange(k)
    return np.exp2(a[idx // 512, idx % 128 // 32])


BF16 = ml_dtypes.bfloat16


def bf(x):
    return np.asarray(x, np.float32).astype(BF16)


def f64(x):
    return np.asarray(x).astype(np.float64)


T, K, N = 8192, 1024, 512

Q = 127
IN_GRAN = (1, 32)
W_GRAN = (32, 32)


def on_grid(R, C, gran):
    gr, gc = gran
    k = np.random.randint(-Q, Q + 1, (R // gr, C // gc, gr * gc))
    pos = np.random.randint(0, gr * gc, (R // gr, C // gc, 1))
    sgn = 2 * np.random.randint(0, 2, (R // gr, C // gc, 1)) - 1
    np.put_along_axis(k, pos, Q * sgn, axis=2)
    return f64(k.reshape(R // gr, C // gc, gr, gc).transpose(0, 2, 1, 3).reshape(R, C))


def setup_inputs():
    s = mx_kscale(T)[:, None]
    x = on_grid(T, K, IN_GRAN) * 2.0 ** -6 * s
    weight = on_grid(N, K, W_GRAN) * 2.0 ** -12
    bias = np.random.uniform(-0.5, 0.5, N)
    g = np.random.standard_normal((T, N)) * np.exp2(np.random.randint(-12, 1, (T, 1))) * 0.25 / s
    return {"x": bf(x), "weight": bf(weight), "bias": bf(bias), "grad_out": bf(g)}


def reference(x, weight, bias, grad_out):
    return mxq(f64(grad_out), 0, "e5m2").T @ mxq(f64(x), 0, "e4m3")

@@ -1,0 +1,119 @@
+from contextlib import ExitStack
+
+import concourse.mybir as mybir
+
+BF16 = mybir.dt.bfloat16
+F32 = mybir.dt.float32
+U32 = mybir.dt.uint32
+U8 = mybir.dt.uint8
+E4M3X4 = mybir.dt.float8_e4m3fn_x4
+E5M2X4 = mybir.dt.float8_e5m2_x4
+
+T, K, N = 8192, 1024, 512
+P = 128
+PACK = 4
+T_PASS = P * PACK
+CHUNKS = T // T_PASS
+M_TILES = N // P
+N_TILE = 512
+N_TILES = K // N_TILE
+
+FLOPS = 2 * T * K * N
+BYTES = 2 * T * (K + N) + 4 * N * K
+
+RAW_BUFS = 8
+MID_BUFS = 3
+X_SCALAR_COLS = 768
+MANUAL = False
+
+
+def regroup(engine_copy, dst, src, lo, hi):
+    engine_copy(
+        out=dst[:, lo:hi, :].rearrange("p (c i) t -> p c t i", i=4),
+        in_=src[:, :, lo:hi].rearrange("p t (c i) -> p c t i", i=4),
+    )
+
+
+def tile_linearmem_t_kernel(tc, x, weight, bias, grad_out, out):
+    nc = tc.nc
+    x_v = x.rearrange("(c p j) w -> c p j w", p=P, j=PACK)
+    g_v = grad_out.rearrange("(c p j) w -> c p j w", p=P, j=PACK)
+    with ExitStack() as ctx:
+        if MANUAL:
+            ctx.enter_context(tc.manual_schedule())
+        raw = ctx.enter_context(tc.tile_pool(name="raw", bufs=RAW_BUFS))
+        mid = ctx.enter_context(tc.tile_pool(name="mid", bufs=MID_BUFS))
+        res = ctx.enter_context(tc.tile_pool(name="res", bufs=1))
+        psum = ctx.enter_context(tc.psum_pool(name="psum", bufs=1))
+
+        acc = [
+            [psum.tile([P, N_TILE], F32, name="acc%d_%d" % (m, n)) for n in range(N_TILES)]
+            for m in range(M_TILES)
+        ]
+        raws = {}
+        mids = {}
+
+        def load(c):
+            g_raw = raw.tile([P, PACK, N], BF16, name="g_raw")
+            nc.sync.dma_start(out=g_raw[:], in_=g_v[c])
+            x_raw = raw.tile([P, PACK, K], BF16, name="x_raw")
+            nc.sync.dma_start(out=x_raw[:], in_=x_v[c])
+            raws[c] = (g_raw, x_raw)
+
+        def regroup_chunk(c):
+            g_raw, x_raw = raws[c]
+            x_grp = mid.tile([P, K, PACK], BF16, name="x_grp", align_bytes=64)
+            g_grp = mid.tile([P, N, PACK], BF16, name="g_grp", align_bytes=64)
+            regroup(nc.scalar.copy, x_grp, x_raw, 0, X_SCALAR_COLS)
+            regroup(nc.vector.tensor_copy, g_grp, g_raw, 0, N)
+            regroup(nc.vector.tensor_copy, x_grp, x_raw, X_SCALAR_COLS, K)
+            mids[c] = (g_grp, x_grp)
+
+        def quantise_and_multiply(c):
+            g_grp, x_grp = mids[c]
+            g_codes = mid.tile([P, N], U32, name="g_codes", align_bytes=64)
+            g_scales = mid.tile([P, N], U8, name="g_scales", align_bytes=64)
+            x_codes = mid.tile([P, K], U32, name="x_codes", align_bytes=64)
+            x_scales = mid.tile([P, K], U8, name="x_scales", align_bytes=64)
+            nc.vector.quantize_mx(
+                out=g_codes[:].bitcast(E5M2X4),
+                scales=g_scales[:],
+                in_=g_grp[:].rearrange("p w t -> p (w t)"),
+            )
+            nc.vector.quantize_mx(
+                out=x_codes[:].bitcast(E4M3X4),
+                scales=x_scales[:],
+                in_=x_grp[:].rearrange("p w t -> p (w t)"),
+            )
+            for m in range(M_TILES):
+                for n in range(N_TILES):
+                    nc.tensor.matmul_mx(
+                        out=acc[m][n][:],
+                        lhsT=g_codes[:, m * P : (m + 1) * P].bitcast(E5M2X4),
+                        lhsT_scale=g_scales[:, m * P : (m + 1) * P],
+                        rhs=x_codes[:, n * N_TILE : (n + 1) * N_TILE].bitcast(E4M3X4),
+                        rhs_scale=x_scales[:, n * N_TILE : (n + 1) * N_TILE],
+                        start=(c == 0),
+                        stop=(c == CHUNKS - 1),
+                    )
+
+        for c in range(RAW_BUFS):
+            load(c)
+        for c in range(CHUNKS):
+            regroup_chunk(c)
+            if c + RAW_BUFS < CHUNKS:
+                load(c + RAW_BUFS)
+            if c >= 1:
+                quantise_and_multiply(c - 1)
+        quantise_and_multiply(CHUNKS - 1)
+
+        for m in range(M_TILES):
+            for n in range(N_TILES):
+                o_sb = res.tile([P, N_TILE], F32, name="o_sb%d_%d" % (m, n))
+                if n == 0:
+                    nc.vector.tensor_copy(out=o_sb[:], in_=acc[m][n][:])
+                else:
+                    nc.scalar.copy(out=o_sb[:], in_=acc[m][n][:])
+                nc.sync.dma_start(
+                    out=out[m * P : (m + 1) * P, n * N_TILE : (n + 1) * N_TILE], in_=o_sb[:]
+                )

@@ -24,7 +24,7 @@ BYTES = 2 * T * (K + N) + 4 * N * K
 RAW_BUFS = 8
 MID_BUFS = 3
 X_SCALAR_COLS = 768
-MANUAL = False
+MANUAL = True
 
 
 def regroup(engine_copy, dst, src, lo, hi):

@@ -15,23 +15,24 @@ PACK = 4
 T_PASS = P * PACK
 CHUNKS = T // T_PASS
 M_TILES = N // P
-N_TILE = 512
-N_TILES = K // N_TILE
+PIECE = 512
+X_PIECES = K // PIECE
 
 FLOPS = 2 * T * K * N
 BYTES = 2 * T * (K + N) + 4 * N * K
 
 RAW_BUFS = 8
-MID_BUFS = 3
-X_SCALAR_COLS = 768
-MANUAL = True
+GRP_BUFS = 6
+SCALAR_COLS = 264
+RUN = 4
 
 
-def regroup(engine_copy, dst, src, lo, hi):
-    engine_copy(
-        out=dst[:, lo:hi, :].rearrange("p (c i) t -> p c t i", i=4),
-        in_=src[:, :, lo:hi].rearrange("p t (c i) -> p c t i", i=4),
-    )
+def by_runs_dst(ap):
+    return ap.rearrange("p (c i) t -> p c t i", i=RUN)
+
+
+def by_runs_src(ap):
+    return ap.rearrange("p t (c i) -> p c t i", i=RUN)
 
 
 def tile_linearmem_t_kernel(tc, x, weight, bias, grad_out, out):
@@ -39,19 +40,22 @@ def tile_linearmem_t_kernel(tc, x, weight, bias, grad_out, out):
     x_v = x.rearrange("(c p j) w -> c p j w", p=P, j=PACK)
     g_v = grad_out.rearrange("(c p j) w -> c p j w", p=P, j=PACK)
     with ExitStack() as ctx:
-        if MANUAL:
-            ctx.enter_context(tc.manual_schedule())
+        ctx.enter_context(tc.manual_schedule())
         raw = ctx.enter_context(tc.tile_pool(name="raw", bufs=RAW_BUFS))
-        mid = ctx.enter_context(tc.tile_pool(name="mid", bufs=MID_BUFS))
+        grp_pool = ctx.enter_context(tc.tile_pool(name="grp", bufs=GRP_BUFS))
+        g_pool = ctx.enter_context(tc.tile_pool(name="gq", bufs=3))
+        x_pool = ctx.enter_context(tc.tile_pool(name="xq", bufs=4))
         res = ctx.enter_context(tc.tile_pool(name="res", bufs=1))
         psum = ctx.enter_context(tc.psum_pool(name="psum", bufs=1))
 
         acc = [
-            [psum.tile([P, N_TILE], F32, name="acc%d_%d" % (m, n)) for n in range(N_TILES)]
+            [psum.tile([P, PIECE], F32, name="acc%d_%d" % (m, n)) for n in range(X_PIECES)]
             for m in range(M_TILES)
         ]
+        pieces = [(c, n) for c in range(CHUNKS) for n in range(-1, X_PIECES)]
         raws = {}
-        mids = {}
+        grouped = {}
+        g_quant = {}
 
         def load(c):
             g_raw = raw.tile([P, PACK, N], BF16, name="g_raw")
@@ -60,60 +64,60 @@ def tile_linearmem_t_kernel(tc, x, weight, bias, grad_out, out):
             nc.sync.dma_start(out=x_raw[:], in_=x_v[c])
             raws[c] = (g_raw, x_raw)
 
-        def regroup_chunk(c):
-            g_raw, x_raw = raws[c]
-            x_grp = mid.tile([P, K, PACK], BF16, name="x_grp", align_bytes=64)
-            g_grp = mid.tile([P, N, PACK], BF16, name="g_grp", align_bytes=64)
-            regroup(nc.scalar.copy, x_grp, x_raw, 0, X_SCALAR_COLS)
-            regroup(nc.vector.tensor_copy, g_grp, g_raw, 0, N)
-            regroup(nc.vector.tensor_copy, x_grp, x_raw, X_SCALAR_COLS, K)
-            mids[c] = (g_grp, x_grp)
+        def regroup(i):
+            c, n = pieces[i]
+            src = raws[c][0] if n < 0 else raws[c][1][:, :, n * PIECE : (n + 1) * PIECE]
+            grp = grp_pool.tile([P, PIECE, PACK], BF16, name="grp", align_bytes=64)
+            nc.scalar.copy(
+                out=by_runs_dst(grp[:, 0:SCALAR_COLS, :]), in_=by_runs_src(src[:, :, 0:SCALAR_COLS])
+            )
+            nc.vector.tensor_copy(
+                out=by_runs_dst(grp[:, SCALAR_COLS:PIECE, :]),
+                in_=by_runs_src(src[:, :, SCALAR_COLS:PIECE]),
+            )
+            grouped[i] = grp
 
-        def quantise_and_multiply(c):
-            g_grp, x_grp = mids[c]
-            g_codes = mid.tile([P, N], U32, name="g_codes", align_bytes=64)
-            g_scales = mid.tile([P, N], U8, name="g_scales", align_bytes=64)
-            x_codes = mid.tile([P, K], U32, name="x_codes", align_bytes=64)
-            x_scales = mid.tile([P, K], U8, name="x_scales", align_bytes=64)
+        def quantise(i):
+            c, n = pieces[i]
+            pool = g_pool if n < 0 else x_pool
+            codes = pool.tile([P, PIECE], U32, name="codes", align_bytes=64)
+            scales = pool.tile([P, PIECE], U8, name="scales", align_bytes=64)
             nc.vector.quantize_mx(
-                out=g_codes[:].bitcast(E5M2X4),
-                scales=g_scales[:],
-                in_=g_grp[:].rearrange("p w t -> p (w t)"),
+                out=codes[:].bitcast(E5M2X4 if n < 0 else E4M3X4),
+                scales=scales[:],
+                in_=grouped[i][:].rearrange("p w t -> p (w t)"),
             )
-            nc.vector.quantize_mx(
-                out=x_codes[:].bitcast(E4M3X4),
-                scales=x_scales[:],
-                in_=x_grp[:].rearrange("p w t -> p (w t)"),
-            )
+            if n < 0:
+                g_quant[c] = (codes, scales)
+                return
+            g_codes, g_scales = g_quant[c]
             for m in range(M_TILES):
-                for n in range(N_TILES):
-                    nc.tensor.matmul_mx(
-                        out=acc[m][n][:],
-                        lhsT=g_codes[:, m * P : (m + 1) * P].bitcast(E5M2X4),
-                        lhsT_scale=g_scales[:, m * P : (m + 1) * P],
-                        rhs=x_codes[:, n * N_TILE : (n + 1) * N_TILE].bitcast(E4M3X4),
-                        rhs_scale=x_scales[:, n * N_TILE : (n + 1) * N_TILE],
-                        start=(c == 0),
-                        stop=(c == CHUNKS - 1),
-                    )
+                nc.tensor.matmul_mx(
+                    out=acc[m][n][:],
+                    lhsT=g_codes[:, m * P : (m + 1) * P].bitcast(E5M2X4),
+                    lhsT_scale=g_scales[:, m * P : (m + 1) * P],
+                    rhs=codes[:].bitcast(E4M3X4),
+                    rhs_scale=scales[:],
+                    start=(c == 0),
+                    stop=(c == CHUNKS - 1),
+                )
 
         for c in range(RAW_BUFS):
             load(c)
-        for c in range(CHUNKS):
-            regroup_chunk(c)
-            if c + RAW_BUFS < CHUNKS:
+        for i in range(len(pieces)):
+            regroup(i)
+            c, n = pieces[i]
+            if n == X_PIECES - 1 and c + RAW_BUFS < CHUNKS:
                 load(c + RAW_BUFS)
-            if c >= 1:
-                quantise_and_multiply(c - 1)
-        quantise_and_multiply(CHUNKS - 1)
+            if i >= 1:
+                quantise(i - 1)
+        quantise(len(pieces) - 1)
 
-        for m in range(M_TILES):
-            for n in range(N_TILES):
-                o_sb = res.tile([P, N_TILE], F32, name="o_sb%d_%d" % (m, n))
-                if n == 0:
-                    nc.vector.tensor_copy(out=o_sb[:], in_=acc[m][n][:])
-                else:
-                    nc.scalar.copy(out=o_sb[:], in_=acc[m][n][:])
-                nc.sync.dma_start(
-                    out=out[m * P : (m + 1) * P, n * N_TILE : (n + 1) * N_TILE], in_=o_sb[:]
-                )
+        closing = [(m, n) for n in range(X_PIECES) for m in range(M_TILES)]
+        for k, (m, n) in enumerate(closing):
+            o_sb = res.tile([P, PIECE], F32, name="o_sb%d_%d" % (m, n))
+            if k % 2 == 0:
+                nc.scalar.copy(out=o_sb[:], in_=acc[m][n][:])
+            else:
+                nc.vector.tensor_copy(out=o_sb[:], in_=acc[m][n][:])
+            nc.sync.dma_start(out=out[m * P : (m + 1) * P, n * PIECE : (n + 1) * PIECE], in_=o_sb[:])

@@ -23,16 +23,17 @@ BYTES = 2 * T * (K + N) + 4 * N * K
 
 RAW_BUFS = 8
 GRP_BUFS = 6
-SCALAR_COLS = 264
-RUN = 4
+SCALAR_COLS = {-1: 264, 0: 272, 1: 272}
+SCALAR_RUN = 8
+VECTOR_RUN = 4
 
 
-def by_runs_dst(ap):
-    return ap.rearrange("p (c i) t -> p c t i", i=RUN)
+def by_runs_dst(ap, run):
+    return ap.rearrange("p (c i) t -> p c t i", i=run)
 
 
-def by_runs_src(ap):
-    return ap.rearrange("p t (c i) -> p c t i", i=RUN)
+def by_runs_src(ap, run):
+    return ap.rearrange("p t (c i) -> p c t i", i=run)
 
 
 def tile_linearmem_t_kernel(tc, x, weight, bias, grad_out, out):
@@ -68,12 +69,13 @@ def tile_linearmem_t_kernel(tc, x, weight, bias, grad_out, out):
             c, n = pieces[i]
             src = raws[c][0] if n < 0 else raws[c][1][:, :, n * PIECE : (n + 1) * PIECE]
             grp = grp_pool.tile([P, PIECE, PACK], BF16, name="grp", align_bytes=64)
+            cut = SCALAR_COLS[n]
             nc.scalar.copy(
-                out=by_runs_dst(grp[:, 0:SCALAR_COLS, :]), in_=by_runs_src(src[:, :, 0:SCALAR_COLS])
+                out=by_runs_dst(grp[:, 0:cut, :], SCALAR_RUN), in_=by_runs_src(src[:, :, 0:cut], SCALAR_RUN)
             )
             nc.vector.tensor_copy(
-                out=by_runs_dst(grp[:, SCALAR_COLS:PIECE, :]),
-                in_=by_runs_src(src[:, :, SCALAR_COLS:PIECE]),
+                out=by_runs_dst(grp[:, cut:PIECE, :], VECTOR_RUN),
+                in_=by_runs_src(src[:, :, cut:PIECE], VECTOR_RUN),
             )
             grouped[i] = grp
 

from contextlib import ExitStack

import concourse.mybir as mybir

BF16 = mybir.dt.bfloat16
F32 = mybir.dt.float32
U32 = mybir.dt.uint32
U8 = mybir.dt.uint8
E4M3X4 = mybir.dt.float8_e4m3fn_x4
E5M2X4 = mybir.dt.float8_e5m2_x4

T, K, N = 8192, 1024, 512
P = 128
PACK = 4
T_PASS = P * PACK
CHUNKS = T // T_PASS
M_TILES = N // P
PIECE = 512
X_PIECES = K // PIECE

FLOPS = 2 * T * K * N
BYTES = 2 * T * (K + N) + 4 * N * K

RAW_BUFS = 8
GRP_BUFS = 6
SCALAR_COLS = {-1: 264, 0: 272, 1: 272}
SCALAR_RUN = 8
VECTOR_RUN = 4


def by_runs_dst(ap, run):
    return ap.rearrange("p (c i) t -> p c t i", i=run)


def by_runs_src(ap, run):
    return ap.rearrange("p t (c i) -> p c t i", i=run)


def tile_linearmem_t_kernel(tc, x, weight, bias, grad_out, out):
    nc = tc.nc
    x_v = x.rearrange("(c p j) w -> c p j w", p=P, j=PACK)
    g_v = grad_out.rearrange("(c p j) w -> c p j w", p=P, j=PACK)
    with ExitStack() as ctx:
        ctx.enter_context(tc.manual_schedule())
        raw = ctx.enter_context(tc.tile_pool(name="raw", bufs=RAW_BUFS))
        grp_pool = ctx.enter_context(tc.tile_pool(name="grp", bufs=GRP_BUFS))
        g_pool = ctx.enter_context(tc.tile_pool(name="gq", bufs=3))
        x_pool = ctx.enter_context(tc.tile_pool(name="xq", bufs=4))
        res = ctx.enter_context(tc.tile_pool(name="res", bufs=1))
        psum = ctx.enter_context(tc.psum_pool(name="psum", bufs=1))

        acc = [
            [psum.tile([P, PIECE], F32, name="acc%d_%d" % (m, n)) for n in range(X_PIECES)]
            for m in range(M_TILES)
        ]
        pieces = [(c, n) for c in range(CHUNKS) for n in range(-1, X_PIECES)]
        raws = {}
        grouped = {}
        g_quant = {}

        def load(c):
            g_raw = raw.tile([P, PACK, N], BF16, name="g_raw")
            nc.sync.dma_start(out=g_raw[:], in_=g_v[c])
            x_raw = raw.tile([P, PACK, K], BF16, name="x_raw")
            nc.sync.dma_start(out=x_raw[:], in_=x_v[c])
            raws[c] = (g_raw, x_raw)

        def regroup(i):
            c, n = pieces[i]
            src = raws[c][0] if n < 0 else raws[c][1][:, :, n * PIECE : (n + 1) * PIECE]
            grp = grp_pool.tile([P, PIECE, PACK], BF16, name="grp", align_bytes=64)
            cut = SCALAR_COLS[n]
            nc.scalar.copy(
                out=by_runs_dst(grp[:, 0:cut, :], SCALAR_RUN), in_=by_runs_src(src[:, :, 0:cut], SCALAR_RUN)
            )
            nc.vector.tensor_copy(
                out=by_runs_dst(grp[:, cut:PIECE, :], VECTOR_RUN),
                in_=by_runs_src(src[:, :, cut:PIECE], VECTOR_RUN),
            )
            grouped[i] = grp

        def quantise(i):
            c, n = pieces[i]
            pool = g_pool if n < 0 else x_pool
            codes = pool.tile([P, PIECE], U32, name="codes", align_bytes=64)
            scales = pool.tile([P, PIECE], U8, name="scales", align_bytes=64)
            nc.vector.quantize_mx(
                out=codes[:].bitcast(E5M2X4 if n < 0 else E4M3X4),
                scales=scales[:],
                in_=grouped[i][:].rearrange("p w t -> p (w t)"),
            )
            if n < 0:
                g_quant[c] = (codes, scales)
                return
            g_codes, g_scales = g_quant[c]
            for m in range(M_TILES):
                nc.tensor.matmul_mx(
                    out=acc[m][n][:],
                    lhsT=g_codes[:, m * P : (m + 1) * P].bitcast(E5M2X4),
                    lhsT_scale=g_scales[:, m * P : (m + 1) * P],
                    rhs=codes[:].bitcast(E4M3X4),
                    rhs_scale=scales[:],
                    start=(c == 0),
                    stop=(c == CHUNKS - 1),
                )

        for c in range(RAW_BUFS):
            load(c)
        for i in range(len(pieces)):
            regroup(i)
            c, n = pieces[i]
            if n == X_PIECES - 1 and c + RAW_BUFS < CHUNKS:
                load(c + RAW_BUFS)
            if i >= 1:
                quantise(i - 1)
        quantise(len(pieces) - 1)

        closing = [(m, n) for n in range(X_PIECES) for m in range(M_TILES)]
        for k, (m, n) in enumerate(closing):
            o_sb = res.tile([P, PIECE], F32, name="o_sb%d_%d" % (m, n))
            if k % 2 == 0:
                nc.scalar.copy(out=o_sb[:], in_=acc[m][n][:])
            else:
                nc.vector.tensor_copy(out=o_sb[:], in_=acc[m][n][:])
            nc.sync.dma_start(out=out[m * P : (m + 1) * P, n * PIECE : (n + 1) * PIECE], in_=o_sb[:])
